import numpy as np
import ml_dtypes


BF16 = ml_dtypes.bfloat16


def bf(x):
    return np.asarray(x, np.float32).astype(BF16)


def f64(x):
    return np.asarray(x).astype(np.float64)


E2M1 = np.array([0.0, 0.5, 1.0, 1.5, 2.0, 3.0, 4.0, 6.0, -0.0, -0.5, -1.0, -1.5, -2.0, -3.0, -4.0, -6.0])


def pack_weight(w, fmt):
    k, n = w.shape
    w = f64(bf(w)).reshape(k // 32, 32, n)
    amax = np.abs(w).max(1)
    if fmt == "e4m3":
        byte = np.frexp(amax)[1] - 1 + 127 - 7
    else:
        mant, ex = np.frexp(amax / 6.0)
        byte = np.where(mant > 0.5, ex, ex - 1) + 127
    byte = np.clip(np.where(amax > 0, byte, 1), 1, 254)
    scaled = (w * np.exp2(127.0 - byte)[:, None, :]).reshape(k, n).astype(np.float32)
    by_word = np.ascontiguousarray(scaled.reshape(k // 512, 128, 4, n).transpose(0, 1, 3, 2))
    if fmt == "e4m3":
        words = by_word.astype(ml_dtypes.float8_e4m3fn).view(np.uint8)
    else:
        c = by_word.astype(ml_dtypes.float4_e2m1fn).view(np.uint8) & 0xF
        words = c[..., 0::2] | (c[..., 1::2] << 4)
    return np.ascontiguousarray(words), np.ascontiguousarray(byte.astype(np.uint8).reshape(k // 512, 16, n))


def unpack_weight(words, scales, fmt):
    g, p, n, _ = words.shape
    if fmt == "e4m3":
        vals = np.ascontiguousarray(words).view(ml_dtypes.float8_e4m3fn).astype(np.float64)
    else:
        nib = np.empty((g, p, n, 4), np.uint8)
        nib[..., 0::2] = words & 0xF
        nib[..., 1::2] = words >> 4
        vals = E2M1[nib]
    vals = vals * np.repeat(np.exp2(scales.astype(np.float64) - 127.0), 8, axis=1)[..., None]
    return vals.transpose(0, 1, 3, 2).reshape(g * 512, n)

def pack4(w):
    words, scales = pack_weight(w, "e2m1")
    return words.reshape(words.shape[0], 128, -1), scales


def unpack4(words, scales):
    return unpack_weight(words.reshape(words.shape[0], 128, -1, 2), scales, "e2m1")


def kspread(k):
    return np.exp2(np.repeat(np.random.randint(-6, 7, k // 32), 32).astype(np.float64))


B, S, HIDDEN, NH, NKV, HD, WINDOW = 1, 512, 3072, 8, 4, 128, 512
Q_SIZE, KV_SIZE = NH * HD, NKV * HD
O_SIZE = Q_SIZE + KV_SIZE + KV_SIZE
EPS = 1e-6
ROPE_THETA = 10000.0


def rms_norm(u, w):
    var = np.mean(np.square(u), axis=-1, keepdims=True)
    return u / np.sqrt(var + EPS) * (1.0 + w)


def rope(u, cos, sin):
    d2 = u.shape[-1] // 2
    u1, u2 = u[..., :d2], u[..., d2:]
    c = cos[None, :, None, :]
    s = sin[None, :, None, :]
    return np.concatenate([u1 * c - u2 * s, u1 * s + u2 * c], axis=-1)


def setup_inputs():
    s = kspread(HIDDEN)
    inv_freq = 1.0 / ROPE_THETA ** (np.arange(0, HD, 2) / HD)
    ang = np.arange(S)[:, None] * inv_freq[None, :]
    x = np.random.standard_normal((B, S, HIDDEN)) * s
    x_words, x_scales = pack4(np.ascontiguousarray(x.reshape(B * S, HIDDEN).T))
    qkv_w = np.random.standard_normal((O_SIZE, HIDDEN)) / np.sqrt(HIDDEN) / s[None, :]
    words, scales = pack4(np.ascontiguousarray(qkv_w.T))
    return {"x_words": x_words,
            "x_scales": x_scales,
            "qkv_w_words": words,
            "qkv_w_scales": scales,
            "q_norm_w": bf(1.0 + 0.3 * np.random.standard_normal(HD)),
            "k_norm_w": bf(1.0 + 0.3 * np.random.standard_normal(HD)),
            "freqs_cos": bf(np.cos(ang)),
            "freqs_sin": bf(np.sin(ang))}


def reference(x_words, x_scales, qkv_w_words, qkv_w_scales, q_norm_w, k_norm_w, freqs_cos, freqs_sin):
    xq = unpack4(x_words, x_scales).T.reshape(B, S, HIDDEN)
    qkv = xq @ unpack4(qkv_w_words, qkv_w_scales)
    q = qkv[..., :Q_SIZE].reshape(B, S, NH, HD)
    k = qkv[..., Q_SIZE:Q_SIZE + KV_SIZE].reshape(B, S, NKV, HD)
    v = qkv[..., Q_SIZE + KV_SIZE:].reshape(B, S, NKV, HD)
    q = rms_norm(q, f64(q_norm_w))
    k = rms_norm(k, f64(k_norm_w))
    q = rope(q, f64(freqs_cos), f64(freqs_sin))
    k = rope(k, f64(freqs_cos), f64(freqs_sin))
    return q, k, v

@@ -1,0 +1,212 @@
+from contextlib import ExitStack
+import math
+
+import concourse.mybir as mybir
+
+F32 = mybir.dt.float32
+BF16 = mybir.dt.bfloat16
+I32 = mybir.dt.int32
+U8 = mybir.dt.uint8
+FP4X4 = mybir.dt.float4_e2m1fn_x4
+ACT = mybir.ActivationFunctionType
+ALU = mybir.AluOpType
+
+P = 128
+TOKENS = 512
+HIDDEN = 3072
+COLS = 2048
+PASSES = HIDDEN // 512
+TB = TOKENS // P
+NB = 512
+CB = COLS // NB
+HD = 128
+HALF = HD // 2
+EPS = 1e-6
+FLOPS = 2 * TOKENS * HIDDEN * COLS
+
+N_WARM = 8
+G_OUTER = 3
+
+
+def tile_gemmaattention_pa_kernel(
+    tc, x_words, x_scales, qkv_w_words, qkv_w_scales, q_norm_w, k_norm_w, freqs_cos, freqs_sin, out_0, out_1, out_2
+):
+    nc = tc.nc
+    q_out = out_0.rearrange("b s h d -> (b s) (h d)")
+    k_out = out_1.rearrange("b s h d -> (b s) (h d)")
+    v_out = out_2.rearrange("b s h d -> (b s) (h d)")
+
+    with ExitStack() as ctx:
+        keep = ctx.enter_context(tc.tile_pool(name="keep", bufs=1))
+        work = ctx.enter_context(tc.tile_pool(name="work", bufs=4))
+        outs = ctx.enter_context(tc.tile_pool(name="outs", bufs=6))
+        psum = ctx.enter_context(tc.psum_pool(name="psum", bufs=8))
+        ctx.enter_context(tc.manual_schedule())
+
+        xs = keep.tile([P, PASSES, TOKENS], U8, name="xs", align_bytes=64)
+        ws = []
+        for cb in range(CB):
+            ws_cb = keep.tile([P, PASSES, NB], U8, name="ws%d" % cb, align_bytes=64)
+            ws.append(ws_cb)
+        warm = keep.tile([P, NB], BF16, name="warm")
+        wrow = keep.tile([P, 2 * HD], BF16, name="wrow")
+        eps = keep.tile([P, 1], F32, name="eps")
+        junk = keep.tile([P, HD], F32, name="junk")
+        cos = keep.tile([P, TB, HALF], BF16, name="cos")
+        sin = keep.tile([P, TB, HALF], BF16, name="sin")
+        gain = keep.tile([P, 2 * HD], F32, name="gain")
+        tab_c = keep.tile([P, TB, 2, HD], F32, name="tab_c")
+        tab_s = keep.tile([P, TB, 2, HD], F32, name="tab_s")
+
+        xc = {}
+        wc = {}
+
+        def load_x(g0, g1):
+            t = keep.tile([P, g1 - g0, 2 * TOKENS], U8, name="xc%d" % g0, align_bytes=64)
+            nc.sync.dma_start(
+                out=t[:].bitcast(I32), in_=x_words[g0:g1].rearrange("g p n -> p g n").bitcast(I32)
+            )
+            for g in range(g0, g1):
+                xc[g] = t[:, g - g0, :]
+
+        def load_w(cb, g0, g1):
+            t = keep.tile([P, g1 - g0, 2 * NB], U8, name="wc%d_%d" % (cb, g0), align_bytes=64)
+            nc.sync.dma_start(
+                out=t[:].bitcast(I32),
+                in_=qkv_w_words[g0:g1, :, 2 * NB * cb : 2 * NB * (cb + 1)].rearrange("g p n -> p g n").bitcast(I32),
+            )
+            for g in range(g0, g1):
+                wc[(g, cb)] = t[:, g - g0, :]
+
+        def load_scales(plane, src):
+            for quad in range(4):
+                nc.sync.dma_start(
+                    out=plane[32 * quad : 32 * quad + 4, :, :].bitcast(I32),
+                    in_=src[:, 4 * quad : 4 * quad + 4, :].rearrange("g r n -> r g n").bitcast(I32),
+                )
+
+        nc.vector.memset(xs[:].bitcast(I32), 0)
+        nc.vector.memset(ws[0][:].bitcast(I32), 0)
+        nc.vector.memset(warm[:], 1.0)
+        nc.vector.memset(wrow[:], 0.0)
+        nc.vector.memset(eps[:], EPS)
+        for cb in range(1, CB):
+            nc.vector.memset(ws[cb][:].bitcast(I32), 0)
+
+        nc.gpsimd.dma_start(out=wrow[0:1, 0:HD], in_=q_norm_w.rearrange("(o n) -> o n", o=1))
+        nc.gpsimd.dma_start(out=wrow[0:1, HD : 2 * HD], in_=k_norm_w.rearrange("(o n) -> o n", o=1))
+        nc.gpsimd.dma_start(out=cos[:], in_=freqs_cos.rearrange("(t p) d -> p t d", p=P))
+        nc.gpsimd.dma_start(out=sin[:], in_=freqs_sin.rearrange("(t p) d -> p t d", p=P))
+
+        load_x(0, 1)
+        load_w(0, 0, 1)
+        load_scales(xs, x_scales)
+        load_scales(ws[0], qkv_w_scales[:, :, 0:NB])
+        load_x(1, 3)
+        load_w(0, 1, 3)
+        load_x(3, 6)
+        load_w(0, 3, 6)
+        for cb in range(1, CB):
+            load_scales(ws[cb], qkv_w_scales[:, :, NB * cb : NB * (cb + 1)])
+            load_w(cb, 0, 3)
+            load_w(cb, 3, 6)
+
+        nc.scalar.activation(out=junk[:, 0:1], in_=eps[:], func=ACT.Abs_reciprocal_sqrt)
+
+        warm_ps = psum.tile([P, NB], F32, name="warm_ps", tag="acc")
+        for i in range(N_WARM):
+            nc.tensor.matmul(out=warm_ps[:], lhsT=warm[:, 0:P], rhs=warm[:], start=True, stop=True)
+
+        def mm(acc, g, tb, cb, c0, n):
+            nc.tensor.matmul_mx(
+                out=acc,
+                lhsT=xc[g][:, 2 * P * tb : 2 * P * (tb + 1)].bitcast(FP4X4),
+                lhsT_scale=xs[:, g, P * tb : P * (tb + 1)],
+                rhs=wc[(g, cb)][:, 2 * c0 : 2 * (c0 + n)].bitcast(FP4X4),
+                rhs_scale=ws[cb][:, g, c0 : c0 + n],
+                start=(g == 0),
+                stop=(g == PASSES - 1),
+            )
+
+        def norm_rope(acc, tb, cb):
+            which = 0 if cb < 2 else 1
+            ms = work.tile([P, 4], F32, name="ms", tag="ms")
+            for h in range(4):
+                nc.scalar.activation(
+                    out=junk[:],
+                    in_=acc[:, HD * h : HD * (h + 1)],
+                    func=ACT.Square,
+                    scale=1.0 / math.sqrt(HD),
+                    accum_out=ms[:, h : h + 1],
+                )
+            rstd = work.tile([P, 4], F32, name="rstd", tag="rstd")
+            nc.scalar.activation(out=rstd[:], in_=ms[:], func=ACT.Abs_reciprocal_sqrt, bias=eps[:, 0:1], scale=1.0)
+            uc = work.tile([P, NB], F32, name="uc", tag="uc")
+            us = work.tile([P, NB], F32, name="us", tag="us")
+            for h in range(4):
+                cols = slice(HD * h, HD * (h + 1))
+                nc.vector.scalar_tensor_tensor(
+                    out=uc[:, cols], in0=acc[:, cols], scalar=rstd[:, h : h + 1], in1=tab_c[:, tb, which, :],
+                    op0=ALU.mult, op1=ALU.mult,
+                )
+                nc.vector.scalar_tensor_tensor(
+                    out=us[:, cols], in0=acc[:, cols], scalar=rstd[:, h : h + 1], in1=tab_s[:, tb, which, :],
+                    op0=ALU.mult, op1=ALU.mult,
+                )
+            res = outs.tile([P, NB], F32, name="res", tag="res")
+            r4 = res[:].rearrange("p (h t d) -> p h t d", t=2, d=HALF)
+            c4 = uc[:].rearrange("p (h t d) -> p h t d", t=2, d=HALF)
+            s4 = us[:].rearrange("p (h t d) -> p h t d", t=2, d=HALF)
+            nc.gpsimd.tensor_tensor(out=r4[:, :, 0, :], in0=c4[:, :, 0, :], in1=s4[:, :, 1, :], op=ALU.subtract)
+            nc.gpsimd.tensor_tensor(out=r4[:, :, 1, :], in0=c4[:, :, 1, :], in1=s4[:, :, 0, :], op=ALU.add)
+            rows = slice(P * tb, P * (tb + 1))
+            if cb < 2:
+                nc.sync.dma_start(out=q_out[rows, NB * cb : NB * (cb + 1)], in_=res[:])
+            else:
+                nc.sync.dma_start(out=k_out[rows, :], in_=res[:])
+
+        first = []
+        for tb in range(TB):
+            acc = psum.tile([P, NB], F32, name="acc", tag="acc")
+            first.append(acc)
+        for g in range(G_OUTER):
+            for tb in range(TB):
+                mm(first[tb][:], g, tb, 0, 0, NB)
+            if g == 0:
+                gain_ps = psum.tile([P, 2 * HD], F32, name="gain_ps", tag="acc")
+                nc.tensor.matmul(out=gain_ps[:], lhsT=warm[:, 0:P], rhs=wrow[:], start=True, stop=True)
+                nc.vector.tensor_scalar(out=gain[:], in0=gain_ps[:], scalar1=1.0, scalar2=None, op0=ALU.add)
+                g4 = gain[:].rearrange("p (a d) -> p a d", d=HALF)
+                for tb in range(TB):
+                    nc.vector.tensor_tensor(
+                        out=tab_c[:, tb].rearrange("p q (h d) -> p (q h) d", d=HALF), in0=g4,
+                        in1=cos[:, tb, :].unsqueeze(1).to_broadcast([P, 4, HALF]), op=ALU.mult,
+                    )
+                    nc.vector.tensor_tensor(
+                        out=tab_s[:, tb].rearrange("p q (h d) -> p (q h) d", d=HALF), in0=g4,
+                        in1=sin[:, tb, :].unsqueeze(1).to_broadcast([P, 4, HALF]), op=ALU.mult,
+                    )
+        for tb in range(TB):
+            for g in range(G_OUTER, PASSES):
+                mm(first[tb][:], g, tb, 0, 0, NB)
+            norm_rope(first[tb], tb, 0)
+
+        for cb in (1, 2):
+            for tb in range(TB):
+                acc = psum.tile([P, NB], F32, name="acc", tag="acc")
+                for g in range(PASSES):
+                    mm(acc[:], g, tb, cb, 0, NB)
+                norm_rope(acc, tb, cb)
+
+        for tb in range(TB):
+            rows = slice(P * tb, P * (tb + 1))
+            widths = [NB] if tb < TB - 1 else [NB // 2, NB // 2]
+            c0 = 0
+            for n in widths:
+                acc = psum.tile([P, n], F32, name="acc", tag="acc")
+                for g in range(PASSES):
+                    mm(acc[:], g, tb, 3, c0, n)
+                res = outs.tile([P, n], F32, name="res", tag="res")
+                nc.scalar.copy(out=res[:], in_=acc[:])
+                nc.sync.dma_start(out=v_out[rows, c0 : c0 + n], in_=res[:])
+                c0 += n

@@ -24,7 +24,7 @@ HALF = HD // 2
 EPS = 1e-6
 FLOPS = 2 * TOKENS * HIDDEN * COLS
 
-N_WARM = 8
+N_WARM = 10
 G_OUTER = 3
 
 
@@ -39,7 +39,7 @@ def tile_gemmaattention_pa_kernel(
     with ExitStack() as ctx:
         keep = ctx.enter_context(tc.tile_pool(name="keep", bufs=1))
         work = ctx.enter_context(tc.tile_pool(name="work", bufs=4))
-        outs = ctx.enter_context(tc.tile_pool(name="outs", bufs=6))
+        vals = ctx.enter_context(tc.tile_pool(name="vals", bufs=5))
         psum = ctx.enter_context(tc.psum_pool(name="psum", bufs=8))
         ctx.enter_context(tc.manual_schedule())
 
@@ -54,7 +54,8 @@ def tile_gemmaattention_pa_kernel(
         junk = keep.tile([P, HD], F32, name="junk")
         cos = keep.tile([P, TB, HALF], BF16, name="cos")
         sin = keep.tile([P, TB, HALF], BF16, name="sin")
-        gain = keep.tile([P, 2 * HD], F32, name="gain")
+        gain_c = keep.tile([P, 2 * HD], F32, name="gain_c")
+        gain_s = keep.tile([P, 2 * HD], F32, name="gain_s")
         tab_c = keep.tile([P, TB, 2, HD], F32, name="tab_c")
         tab_s = keep.tile([P, TB, 2, HD], F32, name="tab_s")
 
@@ -79,24 +80,22 @@ def tile_gemmaattention_pa_kernel(
                 wc[(g, cb)] = t[:, g - g0, :]
 
         def load_scales(plane, src):
-            for quad in range(4):
+            for r in range(4):
                 nc.sync.dma_start(
-                    out=plane[32 * quad : 32 * quad + 4, :, :].bitcast(I32),
-                    in_=src[:, 4 * quad : 4 * quad + 4, :].rearrange("g r n -> r g n").bitcast(I32),
+                    out=plane[r:P:32, :, :].bitcast(I32),
+                    in_=src[:, r:16:4, :].rearrange("g q n -> q g n").bitcast(I32),
                 )
 
+        nc.vector.memset(wrow[:], 0.0)
+        nc.vector.memset(warm[:], 1.0)
         nc.vector.memset(xs[:].bitcast(I32), 0)
         nc.vector.memset(ws[0][:].bitcast(I32), 0)
-        nc.vector.memset(warm[:], 1.0)
-        nc.vector.memset(wrow[:], 0.0)
         nc.vector.memset(eps[:], EPS)
         for cb in range(1, CB):
             nc.vector.memset(ws[cb][:].bitcast(I32), 0)
 
         nc.gpsimd.dma_start(out=wrow[0:1, 0:HD], in_=q_norm_w.rearrange("(o n) -> o n", o=1))
         nc.gpsimd.dma_start(out=wrow[0:1, HD : 2 * HD], in_=k_norm_w.rearrange("(o n) -> o n", o=1))
-        nc.gpsimd.dma_start(out=cos[:], in_=freqs_cos.rearrange("(t p) d -> p t d", p=P))
-        nc.gpsimd.dma_start(out=sin[:], in_=freqs_sin.rearrange("(t p) d -> p t d", p=P))
 
         load_x(0, 1)
         load_w(0, 0, 1)
@@ -106,6 +105,8 @@ def tile_gemmaattention_pa_kernel(
         load_w(0, 1, 3)
         load_x(3, 6)
         load_w(0, 3, 6)
+        nc.sync.dma_start(out=cos[:], in_=freqs_cos.rearrange("(t p) d -> p t d", p=P))
+        nc.sync.dma_start(out=sin[:], in_=freqs_sin.rearrange("(t p) d -> p t d", p=P))
         for cb in range(1, CB):
             load_scales(ws[cb], qkv_w_scales[:, :, NB * cb : NB * (cb + 1)])
             load_w(cb, 0, 3)
@@ -128,42 +129,80 @@ def tile_gemmaattention_pa_kernel(
                 stop=(g == PASSES - 1),
             )
 
-        def norm_rope(acc, tb, cb):
+        def gains():
+            gain_ps = psum.tile([P, 2 * HD], F32, name="gain_ps", tag="acc")
+            nc.tensor.matmul(out=gain_ps[:], lhsT=warm[:, 0:P], rhs=wrow[:], start=True, stop=True)
+            nc.vector.tensor_scalar(out=gain_c[:], in0=gain_ps[:], scalar1=1.0, scalar2=None, op0=ALU.add)
+            p4 = gain_ps[:].rearrange("p (a d) -> p a d", d=HALF)
+            s4 = gain_s[:].rearrange("p (a d) -> p a d", d=HALF)
+            nc.vector.tensor_scalar(out=s4[:, 0:4:2, :], in0=p4[:, 0:4:2, :], scalar1=1.0, scalar2=None, op0=ALU.add)
+            nc.vector.tensor_scalar(
+                out=s4[:, 1:4:2, :], in0=p4[:, 1:4:2, :], scalar1=1.0, scalar2=-1.0, op0=ALU.add, op1=ALU.mult
+            )
+
+        def tables(which):
+            for tab, gain, trig in ((tab_c, gain_c, cos), (tab_s, gain_s, sin)):
+                nc.vector.tensor_tensor(
+                    out=tab[:, :, which, :].rearrange("p t (h d) -> p t h d", d=HALF),
+                    in0=gain[:, HD * which : HD * (which + 1)].rearrange("p (h d) -> p h d", d=HALF)
+                    .unsqueeze(1).to_broadcast([P, TB, 2, HALF]),
+                    in1=trig[:].unsqueeze(2).to_broadcast([P, TB, 2, HALF]),
+                    op=ALU.mult,
+                )
+
+        state = {}
+
+        def stage_a(i, acc, tb, cb):
             which = 0 if cb < 2 else 1
+            uc = work.tile([P, NB], F32, name="uc", tag="uc")
+            us = work.tile([P, NB], F32, name="us", tag="us")
+            a4 = acc[:].rearrange("p (h t d) -> p h t d", t=2, d=HALF)
+            s4 = us[:].rearrange("p (h t d) -> p h t d", t=2, d=HALF)
+            nc.vector.tensor_tensor(
+                out=uc[:].rearrange("p (h e) -> p h e", e=HD), in0=acc[:].rearrange("p (h e) -> p h e", e=HD),
+                in1=tab_c[:, tb, which, :].unsqueeze(1).to_broadcast([P, 4, HD]), op=ALU.mult,
+            )
+            nc.vector.tensor_tensor(
+                out=s4[:, :, 1, :], in0=a4[:, :, 0, :],
+                in1=tab_s[:, tb, which, 0:HALF].unsqueeze(1).to_broadcast([P, 4, HALF]), op=ALU.mult,
+            )
+            nc.vector.tensor_tensor(
+                out=s4[:, :, 0, :], in0=a4[:, :, 1, :],
+                in1=tab_s[:, tb, which, HALF:HD].unsqueeze(1).to_broadcast([P, 4, HALF]), op=ALU.mult,
+            )
             ms = work.tile([P, 4], F32, name="ms", tag="ms")
             for h in range(4):
                 nc.scalar.activation(
-                    out=junk[:],
-                    in_=acc[:, HD * h : HD * (h + 1)],
-                    func=ACT.Square,
-                    scale=1.0 / math.sqrt(HD),
-                    accum_out=ms[:, h : h + 1],
+                    out=junk[:], in_=acc[:, HD * h : HD * (h + 1)], func=ACT.Square,
+                    scale=1.0 / math.sqrt(HD), accum_out=ms[:, h : h + 1],
                 )
             rstd = work.tile([P, 4], F32, name="rstd", tag="rstd")
             nc.scalar.activation(out=rstd[:], in_=ms[:], func=ACT.Abs_reciprocal_sqrt, bias=eps[:, 0:1], scale=1.0)
-            uc = work.tile([P, NB], F32, name="uc", tag="uc")
-            us = work.tile([P, NB], F32, name="us", tag="us")
+            state[i] = [uc, us, rstd, tb, cb]
+
+        def stage_b(i):
+            uc, us = state[i][0], state[i][1]
+            z = work.tile([P, NB], F32, name="z", tag="z")
+            nc.gpsimd.tensor_tensor(out=z[:], in0=uc[:], in1=us[:], op=ALU.add)
+            state[i].append(z)
+
+        def stage_c(i):
+            rstd, tb, cb, z = state[i][2], state[i][3], state[i][4], state[i][5]
+            res = work.tile([P, NB], F32, name="res", tag="res")
             for h in range(4):
                 cols = slice(HD * h, HD * (h + 1))
-                nc.vector.scalar_tensor_tensor(
-                    out=uc[:, cols], in0=acc[:, cols], scalar=rstd[:, h : h + 1], in1=tab_c[:, tb, which, :],
-                    op0=ALU.mult, op1=ALU.mult,
-                )
-                nc.vector.scalar_tensor_tensor(
-                    out=us[:, cols], in0=acc[:, cols], scalar=rstd[:, h : h + 1], in1=tab_s[:, tb, which, :],
-                    op0=ALU.mult, op1=ALU.mult,
-                )
-            res = outs.tile([P, NB], F32, name="res", tag="res")
-            r4 = res[:].rearrange("p (h t d) -> p h t d", t=2, d=HALF)
-            c4 = uc[:].rearrange("p (h t d) -> p h t d", t=2, d=HALF)
-            s4 = us[:].rearrange("p (h t d) -> p h t d", t=2, d=HALF)
-            nc.gpsimd.tensor_tensor(out=r4[:, :, 0, :], in0=c4[:, :, 0, :], in1=s4[:, :, 1, :], op=ALU.subtract)
-            nc.gpsimd.tensor_tensor(out=r4[:, :, 1, :], in0=c4[:, :, 1, :], in1=s4[:, :, 0, :], op=ALU.add)
+                nc.scalar.activation(out=res[:, cols], in_=z[:, cols], func=ACT.Copy, scale=rstd[:, h : h + 1])
             rows = slice(P * tb, P * (tb + 1))
             if cb < 2:
                 nc.sync.dma_start(out=q_out[rows, NB * cb : NB * (cb + 1)], in_=res[:])
             else:
                 nc.sync.dma_start(out=k_out[rows, :], in_=res[:])
+
+        def epilogue(i, acc, tb, cb):
+            stage_a(i, acc, tb, cb)
+            stage_b(i)
+            if i >= 1:
+                stage_c(i - 1)
 
         first = []
         for tb in range(TB):
@@ -172,31 +211,22 @@ def tile_gemmaattention_pa_kernel(
         for g in range(G_OUTER):
             for tb in range(TB):
                 mm(first[tb][:], g, tb, 0, 0, NB)
-            if g == 0:
-                gain_ps = psum.tile([P, 2 * HD], F32, name="gain_ps", tag="acc")
-                nc.tensor.matmul(out=gain_ps[:], lhsT=warm[:, 0:P], rhs=wrow[:], start=True, stop=True)
-                nc.vector.tensor_scalar(out=gain[:], in0=gain_ps[:], scalar1=1.0, scalar2=None, op0=ALU.add)
-                g4 = gain[:].rearrange("p (a d) -> p a d", d=HALF)
-                for tb in range(TB):
-                    nc.vector.tensor_tensor(
-                        out=tab_c[:, tb].rearrange("p q (h d) -> p (q h) d", d=HALF), in0=g4,
-                        in1=cos[:, tb, :].unsqueeze(1).to_broadcast([P, 4, HALF]), op=ALU.mult,
-                    )
-                    nc.vector.tensor_tensor(
-                        out=tab_s[:, tb].rearrange("p q (h d) -> p (q h) d", d=HALF), in0=g4,
-                        in1=sin[:, tb, :].unsqueeze(1).to_broadcast([P, 4, HALF]), op=ALU.mult,
-                    )
+            if g == 1:
+                gains()
+                tables(0)
         for tb in range(TB):
             for g in range(G_OUTER, PASSES):
                 mm(first[tb][:], g, tb, 0, 0, NB)
-            norm_rope(first[tb], tb, 0)
+            epilogue(tb, first[tb], tb, 0)
+        tables(1)
 
         for cb in (1, 2):
             for tb in range(TB):
                 acc = psum.tile([P, NB], F32, name="acc", tag="acc")
                 for g in range(PASSES):
                     mm(acc[:], g, tb, cb, 0, NB)
-                norm_rope(acc, tb, cb)
+                epilogue(TB * cb + tb, acc, tb, cb)
+        stage_c(3 * TB - 1)
 
         for tb in range(TB):
             rows = slice(P * tb, P * (tb + 1))
@@ -206,7 +236,7 @@ def tile_gemmaattention_pa_kernel(
                 acc = psum.tile([P, n], F32, name="acc", tag="acc")
                 for g in range(PASSES):
                     mm(acc[:], g, tb, 3, c0, n)
-                res = outs.tile([P, n], F32, name="res", tag="res")
-                nc.scalar.copy(out=res[:], in_=acc[:])
-                nc.sync.dma_start(out=v_out[rows, c0 : c0 + n], in_=res[:])
+                val = vals.tile([P, n], F32, name="val", tag="val")
+                nc.vector.tensor_copy(out=val[:], in_=acc[:])
+                nc.sync.dma_start(out=v_out[rows, c0 : c0 + n], in_=val[:])
                 c0 += n

@@ -51,11 +51,10 @@ def tile_gemmaattention_pa_kernel(
         warm = keep.tile([P, NB], BF16, name="warm")
         wrow = keep.tile([P, 2 * HD], BF16, name="wrow")
         eps = keep.tile([P, 1], F32, name="eps")
-        junk = keep.tile([P, HD], F32, name="junk")
+        junk = keep.tile([P, 1], F32, name="junk")
         cos = keep.tile([P, TB, HALF], BF16, name="cos")
         sin = keep.tile([P, TB, HALF], BF16, name="sin")
-        gain_c = keep.tile([P, 2 * HD], F32, name="gain_c")
-        gain_s = keep.tile([P, 2 * HD], F32, name="gain_s")
+        gain = keep.tile([P, 2 * HD], F32, name="gain")
         tab_c = keep.tile([P, TB, 2, HD], F32, name="tab_c")
         tab_s = keep.tile([P, TB, 2, HD], F32, name="tab_s")
 
@@ -112,7 +111,7 @@ def tile_gemmaattention_pa_kernel(
             load_w(cb, 0, 3)
             load_w(cb, 3, 6)
 
-        nc.scalar.activation(out=junk[:, 0:1], in_=eps[:], func=ACT.Abs_reciprocal_sqrt)
+        nc.scalar.activation(out=junk[:], in_=eps[:], func=ACT.Abs_reciprocal_sqrt)
 
         warm_ps = psum.tile([P, NB], F32, name="warm_ps", tag="acc")
         for i in range(N_WARM):
@@ -132,16 +131,10 @@ def tile_gemmaattention_pa_kernel(
         def gains():
             gain_ps = psum.tile([P, 2 * HD], F32, name="gain_ps", tag="acc")
             nc.tensor.matmul(out=gain_ps[:], lhsT=warm[:, 0:P], rhs=wrow[:], start=True, stop=True)
-            nc.vector.tensor_scalar(out=gain_c[:], in0=gain_ps[:], scalar1=1.0, scalar2=None, op0=ALU.add)
-            p4 = gain_ps[:].rearrange("p (a d) -> p a d", d=HALF)
-            s4 = gain_s[:].rearrange("p (a d) -> p a d", d=HALF)
-            nc.vector.tensor_scalar(out=s4[:, 0:4:2, :], in0=p4[:, 0:4:2, :], scalar1=1.0, scalar2=None, op0=ALU.add)
-            nc.vector.tensor_scalar(
-                out=s4[:, 1:4:2, :], in0=p4[:, 1:4:2, :], scalar1=1.0, scalar2=-1.0, op0=ALU.add, op1=ALU.mult
-            )
+            nc.vector.tensor_scalar(out=gain[:], in0=gain_ps[:], scalar1=1.0, scalar2=None, op0=ALU.add)
 
         def tables(which):
-            for tab, gain, trig in ((tab_c, gain_c, cos), (tab_s, gain_s, sin)):
+            for tab, trig in ((tab_c, cos), (tab_s, sin)):
                 nc.vector.tensor_tensor(
                     out=tab[:, :, which, :].rearrange("p t (h d) -> p t h d", d=HALF),
                     in0=gain[:, HD * which : HD * (which + 1)].rearrange("p (h d) -> p h d", d=HALF)
@@ -150,59 +143,51 @@ def tile_gemmaattention_pa_kernel(
                     op=ALU.mult,
                 )
 
-        state = {}
+        pair = {}
 
-        def stage_a(i, acc, tb, cb):
+        def epilogue(i, acc, tb, cb):
             which = 0 if cb < 2 else 1
-            uc = work.tile([P, NB], F32, name="uc", tag="uc")
-            us = work.tile([P, NB], F32, name="us", tag="us")
-            a4 = acc[:].rearrange("p (h t d) -> p h t d", t=2, d=HALF)
-            s4 = us[:].rearrange("p (h t d) -> p h t d", t=2, d=HALF)
-            nc.vector.tensor_tensor(
-                out=uc[:].rearrange("p (h e) -> p h e", e=HD), in0=acc[:].rearrange("p (h e) -> p h e", e=HD),
-                in1=tab_c[:, tb, which, :].unsqueeze(1).to_broadcast([P, 4, HD]), op=ALU.mult,
-            )
-            nc.vector.tensor_tensor(
-                out=s4[:, :, 1, :], in0=a4[:, :, 0, :],
-                in1=tab_s[:, tb, which, 0:HALF].unsqueeze(1).to_broadcast([P, 4, HALF]), op=ALU.mult,
-            )
-            nc.vector.tensor_tensor(
-                out=s4[:, :, 0, :], in0=a4[:, :, 1, :],
-                in1=tab_s[:, tb, which, HALF:HD].unsqueeze(1).to_broadcast([P, 4, HALF]), op=ALU.mult,
-            )
+            j = i % 2
+            if j == 0:
+                uc = work.tile([P, 2, NB], F32, name="uc", tag="uc")
+                us = work.tile([P, 2, NB], F32, name="us", tag="us")
+                pair["uc"] = uc
+                pair["us"] = us
+            uc = pair["uc"]
+            us = pair["us"]
+            sq = work.tile([P, NB], F32, name="sq", tag="sq")
             ms = work.tile([P, 4], F32, name="ms", tag="ms")
             for h in range(4):
+                cols = slice(HD * h, HD * (h + 1))
                 nc.scalar.activation(
-                    out=junk[:], in_=acc[:, HD * h : HD * (h + 1)], func=ACT.Square,
+                    out=sq[:, cols], in_=acc[:, cols], func=ACT.Square,
                     scale=1.0 / math.sqrt(HD), accum_out=ms[:, h : h + 1],
                 )
             rstd = work.tile([P, 4], F32, name="rstd", tag="rstd")
             nc.scalar.activation(out=rstd[:], in_=ms[:], func=ACT.Abs_reciprocal_sqrt, bias=eps[:, 0:1], scale=1.0)
-            state[i] = [uc, us, rstd, tb, cb]
-
-        def stage_b(i):
-            uc, us = state[i][0], state[i][1]
-            z = work.tile([P, NB], F32, name="z", tag="z")
-            nc.gpsimd.tensor_tensor(out=z[:], in0=uc[:], in1=us[:], op=ALU.add)
-            state[i].append(z)
-
-        def stage_c(i):
-            rstd, tb, cb, z = state[i][2], state[i][3], state[i][4], state[i][5]
-            res = work.tile([P, NB], F32, name="res", tag="res")
             for h in range(4):
                 cols = slice(HD * h, HD * (h + 1))
-                nc.scalar.activation(out=res[:, cols], in_=z[:, cols], func=ACT.Copy, scale=rstd[:, h : h + 1])
-            rows = slice(P * tb, P * (tb + 1))
-            if cb < 2:
-                nc.sync.dma_start(out=q_out[rows, NB * cb : NB * (cb + 1)], in_=res[:])
-            else:
-                nc.sync.dma_start(out=k_out[rows, :], in_=res[:])
-
-        def epilogue(i, acc, tb, cb):
-            stage_a(i, acc, tb, cb)
-            stage_b(i)
-            if i >= 1:
-                stage_c(i - 1)
+                nc.vector.scalar_tensor_tensor(
+                    out=uc[:, j, cols], in0=acc[:, cols], scalar=rstd[:, h : h + 1], in1=tab_c[:, tb, which, :],
+                    op0=ALU.mult, op1=ALU.mult,
+                )
+                nc.vector.scalar_tensor_tensor(
+                    out=us[:, j, cols], in0=acc[:, cols], scalar=rstd[:, h : h + 1], in1=tab_s[:, tb, which, :],
+                    op0=ALU.mult, op1=ALU.mult,
+                )
+            if j == 1:
+                res = work.tile([P, 2, NB], F32, name="res", tag="res")
+                r4 = res[:].rearrange("p b (h t d) -> p (b h) t d", t=2, d=HALF)
+                c4 = uc[:].rearrange("p b (h t d) -> p (b h) t d", t=2, d=HALF)
+                s4 = us[:].rearrange("p b (h t d) -> p (b h) t d", t=2, d=HALF)
+                nc.gpsimd.tensor_tensor(out=r4[:, :, 0, :], in0=c4[:, :, 0, :], in1=s4[:, :, 1, :], op=ALU.subtract)
+                nc.gpsimd.tensor_tensor(out=r4[:, :, 1, :], in0=c4[:, :, 1, :], in1=s4[:, :, 0, :], op=ALU.add)
+                rows = slice(P * (tb - 1), P * (tb + 1))
+                if cb < 2:
+                    dst = q_out[rows, NB * cb : NB * (cb + 1)]
+                else:
+                    dst = k_out[rows, :]
+                nc.sync.dma_start(out=dst.rearrange("(b p) n -> p b n", p=P), in_=res[:])
 
         first = []
         for tb in range(TB):
@@ -226,7 +211,6 @@ def tile_gemmaattention_pa_kernel(
                 for g in range(PASSES):
                     mm(acc[:], g, tb, cb, 0, NB)
                 epilogue(TB * cb + tb, acc, tb, cb)
-        stage_c(3 * TB - 1)
 
         for tb in range(TB):
             rows = slice(P * tb, P * (tb + 1))

@@ -24,7 +24,7 @@ HALF = HD // 2
 EPS = 1e-6
 FLOPS = 2 * TOKENS * HIDDEN * COLS
 
-N_WARM = 10
+N_WARM = 12
 G_OUTER = 3
 
 
@@ -180,8 +180,9 @@ def tile_gemmaattention_pa_kernel(
                 r4 = res[:].rearrange("p b (h t d) -> p (b h) t d", t=2, d=HALF)
                 c4 = uc[:].rearrange("p b (h t d) -> p (b h) t d", t=2, d=HALF)
                 s4 = us[:].rearrange("p b (h t d) -> p (b h) t d", t=2, d=HALF)
-                nc.gpsimd.tensor_tensor(out=r4[:, :, 0, :], in0=c4[:, :, 0, :], in1=s4[:, :, 1, :], op=ALU.subtract)
-                nc.gpsimd.tensor_tensor(out=r4[:, :, 1, :], in0=c4[:, :, 1, :], in1=s4[:, :, 0, :], op=ALU.add)
+                eng = nc.vector if i == 3 * TB - 1 else nc.gpsimd
+                eng.tensor_tensor(out=r4[:, :, 0, :], in0=c4[:, :, 0, :], in1=s4[:, :, 1, :], op=ALU.subtract)
+                eng.tensor_tensor(out=r4[:, :, 1, :], in0=c4[:, :, 1, :], in1=s4[:, :, 0, :], op=ALU.add)
                 rows = slice(P * (tb - 1), P * (tb + 1))
                 if cb < 2:
                     dst = q_out[rows, NB * cb : NB * (cb + 1)]

@@ -55,8 +55,9 @@ def tile_gemmaattention_pa_kernel(
         cos = keep.tile([P, TB, HALF], BF16, name="cos")
         sin = keep.tile([P, TB, HALF], BF16, name="sin")
         gain = keep.tile([P, 2 * HD], F32, name="gain")
-        tab_c = keep.tile([P, TB, 2, HD], F32, name="tab_c")
-        tab_s = keep.tile([P, TB, 2, HD], F32, name="tab_s")
+        tab_q = keep.tile([P, TB, 2, HD], F32, name="tab_q")
+        tab_k = keep.tile([P, TB, 2, HD], F32, name="tab_k")
+        tab = (tab_q, tab_k)
 
         xc = {}
         wc = {}
@@ -134,9 +135,9 @@ def tile_gemmaattention_pa_kernel(
             nc.vector.tensor_scalar(out=gain[:], in0=gain_ps[:], scalar1=1.0, scalar2=None, op0=ALU.add)
 
         def tables(which):
-            for tab, trig in ((tab_c, cos), (tab_s, sin)):
+            for cs, trig in ((0, cos), (1, sin)):
                 nc.vector.tensor_tensor(
-                    out=tab[:, :, which, :].rearrange("p t (h d) -> p t h d", d=HALF),
+                    out=tab[which][:, :, cs, :].rearrange("p t (h d) -> p t h d", d=HALF),
                     in0=gain[:, HD * which : HD * (which + 1)].rearrange("p (h d) -> p h d", d=HALF)
                     .unsqueeze(1).to_broadcast([P, TB, 2, HALF]),
                     in1=trig[:].unsqueeze(2).to_broadcast([P, TB, 2, HALF]),
@@ -149,12 +150,9 @@ def tile_gemmaattention_pa_kernel(
             which = 0 if cb < 2 else 1
             j = i % 2
             if j == 0:
-                uc = work.tile([P, 2, NB], F32, name="uc", tag="uc")
-                us = work.tile([P, 2, NB], F32, name="us", tag="us")
-                pair["uc"] = uc
-                pair["us"] = us
-            uc = pair["uc"]
-            us = pair["us"]
+                prod = work.tile([P, 2, 4, 2, HD], F32, name="prod", tag="prod")
+                pair["prod"] = prod
+            prod = pair["prod"]
             sq = work.tile([P, NB], F32, name="sq", tag="sq")
             ms = work.tile([P, 4], F32, name="ms", tag="ms")
             for h in range(4):
@@ -168,18 +166,16 @@ def tile_gemmaattention_pa_kernel(
             for h in range(4):
                 cols = slice(HD * h, HD * (h + 1))
                 nc.vector.scalar_tensor_tensor(
-                    out=uc[:, j, cols], in0=acc[:, cols], scalar=rstd[:, h : h + 1], in1=tab_c[:, tb, which, :],
-                    op0=ALU.mult, op1=ALU.mult,
-                )
-                nc.vector.scalar_tensor_tensor(
-                    out=us[:, j, cols], in0=acc[:, cols], scalar=rstd[:, h : h + 1], in1=tab_s[:, tb, which, :],
+                    out=prod[:, j, h, :, :], in0=acc[:, cols].unsqueeze(1).to_broadcast([P, 2, HD]),
+                    scalar=rstd[:, h : h + 1], in1=tab[which][:, tb, :, :],
                     op0=ALU.mult, op1=ALU.mult,
                 )
             if j == 1:
                 res = work.tile([P, 2, NB], F32, name="res", tag="res")
                 r4 = res[:].rearrange("p b (h t d) -> p (b h) t d", t=2, d=HALF)
-                c4 = uc[:].rearrange("p b (h t d) -> p (b h) t d", t=2, d=HALF)
-                s4 = us[:].rearrange("p b (h t d) -> p (b h) t d", t=2, d=HALF)
+                v5 = prod[:].rearrange("p b h c (t d) -> p (b h) c t d", t=2)
+                c4 = v5[:, :, 0, :, :]
+                s4 = v5[:, :, 1, :, :]
                 eng = nc.vector if i == 3 * TB - 1 else nc.gpsimd
                 eng.tensor_tensor(out=r4[:, :, 0, :], in0=c4[:, :, 0, :], in1=s4[:, :, 1, :], op=ALU.subtract)
                 eng.tensor_tensor(out=r4[:, :, 1, :], in0=c4[:, :, 1, :], in1=s4[:, :, 0, :], op=ALU.add)

@@ -218,6 +218,6 @@ def tile_gemmaattention_pa_kernel(
                 for g in range(PASSES):
                     mm(acc[:], g, tb, 3, c0, n)
                 val = vals.tile([P, n], F32, name="val", tag="val")
-                nc.vector.tensor_copy(out=val[:], in_=acc[:])
-                nc.sync.dma_start(out=v_out[rows, c0 : c0 + n], in_=val[:])
+                nc.scalar.copy(out=val[:], in_=acc[:])
+                nc.scalar.dma_start(out=v_out[rows, c0 : c0 + n], in_=val[:])
                 c0 += n

@@ -176,7 +176,7 @@ def tile_gemmaattention_pa_kernel(
                 v5 = prod[:].rearrange("p b h c (t d) -> p (b h) c t d", t=2)
                 c4 = v5[:, :, 0, :, :]
                 s4 = v5[:, :, 1, :, :]
-                eng = nc.vector if i == 3 * TB - 1 else nc.gpsimd
+                eng = nc.vector if i >= 3 * TB - 3 else nc.gpsimd
                 eng.tensor_tensor(out=r4[:, :, 0, :], in0=c4[:, :, 0, :], in1=s4[:, :, 1, :], op=ALU.subtract)
                 eng.tensor_tensor(out=r4[:, :, 1, :], in0=c4[:, :, 1, :], in1=s4[:, :, 0, :], op=ALU.add)
                 rows = slice(P * (tb - 1), P * (tb + 1))

@@ -193,7 +193,7 @@ def tile_gemmaattention_pa_kernel(
         for g in range(G_OUTER):
             for tb in range(TB):
                 mm(first[tb][:], g, tb, 0, 0, NB)
-            if g == 1:
+            if g == G_OUTER - 1:
                 gains()
                 tables(0)
         for tb in range(TB):

@@ -94,9 +94,6 @@ def tile_gemmaattention_pa_kernel(
         for cb in range(1, CB):
             nc.vector.memset(ws[cb][:].bitcast(I32), 0)
 
-        nc.gpsimd.dma_start(out=wrow[0:1, 0:HD], in_=q_norm_w.rearrange("(o n) -> o n", o=1))
-        nc.gpsimd.dma_start(out=wrow[0:1, HD : 2 * HD], in_=k_norm_w.rearrange("(o n) -> o n", o=1))
-
         load_x(0, 1)
         load_w(0, 0, 1)
         load_scales(xs, x_scales)
@@ -105,6 +102,8 @@ def tile_gemmaattention_pa_kernel(
         load_w(0, 1, 3)
         load_x(3, 6)
         load_w(0, 3, 6)
+        nc.sync.dma_start(out=wrow[0:1, 0:HD], in_=q_norm_w.rearrange("(o n) -> o n", o=1))
+        nc.sync.dma_start(out=wrow[0:1, HD : 2 * HD], in_=k_norm_w.rearrange("(o n) -> o n", o=1))
         nc.sync.dma_start(out=cos[:], in_=freqs_cos.rearrange("(t p) d -> p t d", p=P))
         nc.sync.dma_start(out=sin[:], in_=freqs_sin.rearrange("(t p) d -> p t d", p=P))
         for cb in range(1, CB):

@@ -24,7 +24,7 @@ HALF = HD // 2
 EPS = 1e-6
 FLOPS = 2 * TOKENS * HIDDEN * COLS
 
-N_WARM = 12
+N_WARM = 11
 G_OUTER = 3
 
 
@@ -127,6 +127,17 @@ def tile_gemmaattention_pa_kernel(
                 start=(g == 0),
                 stop=(g == PASSES - 1),
             )
+
+        seen_ps = psum.tile([P, NB], F32, name="seen_ps", tag="acc")
+        nc.tensor.matmul_mx(
+            out=seen_ps[:],
+            lhsT=xc[0][:, 0 : 2 * P].bitcast(FP4X4),
+            lhsT_scale=xs[:, 0, 0:P],
+            rhs=xc[0][:, 0 : 2 * NB].bitcast(FP4X4),
+            rhs_scale=xs[:, 0, 0:NB],
+            start=True,
+            stop=True,
+        )
 
         def gains():
             gain_ps = psum.tile([P, 2 * HD], F32, name="gain_ps", tag="acc")

from contextlib import ExitStack
import math

import concourse.mybir as mybir

F32 = mybir.dt.float32
BF16 = mybir.dt.bfloat16
I32 = mybir.dt.int32
U8 = mybir.dt.uint8
FP4X4 = mybir.dt.float4_e2m1fn_x4
ACT = mybir.ActivationFunctionType
ALU = mybir.AluOpType

P = 128
TOKENS = 512
HIDDEN = 3072
COLS = 2048
PASSES = HIDDEN // 512
TB = TOKENS // P
NB = 512
CB = COLS // NB
HD = 128
HALF = HD // 2
EPS = 1e-6
FLOPS = 2 * TOKENS * HIDDEN * COLS

N_WARM = 11
G_OUTER = 3


def tile_gemmaattention_pa_kernel(
    tc, x_words, x_scales, qkv_w_words, qkv_w_scales, q_norm_w, k_norm_w, freqs_cos, freqs_sin, out_0, out_1, out_2
):
    nc = tc.nc
    q_out = out_0.rearrange("b s h d -> (b s) (h d)")
    k_out = out_1.rearrange("b s h d -> (b s) (h d)")
    v_out = out_2.rearrange("b s h d -> (b s) (h d)")

    with ExitStack() as ctx:
        keep = ctx.enter_context(tc.tile_pool(name="keep", bufs=1))
        work = ctx.enter_context(tc.tile_pool(name="work", bufs=4))
        vals = ctx.enter_context(tc.tile_pool(name="vals", bufs=5))
        psum = ctx.enter_context(tc.psum_pool(name="psum", bufs=8))
        ctx.enter_context(tc.manual_schedule())

        xs = keep.tile([P, PASSES, TOKENS], U8, name="xs", align_bytes=64)
        ws = []
        for cb in range(CB):
            ws_cb = keep.tile([P, PASSES, NB], U8, name="ws%d" % cb, align_bytes=64)
            ws.append(ws_cb)
        warm = keep.tile([P, NB], BF16, name="warm")
        wrow = keep.tile([P, 2 * HD], BF16, name="wrow")
        eps = keep.tile([P, 1], F32, name="eps")
        junk = keep.tile([P, 1], F32, name="junk")
        cos = keep.tile([P, TB, HALF], BF16, name="cos")
        sin = keep.tile([P, TB, HALF], BF16, name="sin")
        gain = keep.tile([P, 2 * HD], F32, name="gain")
        tab_q = keep.tile([P, TB, 2, HD], F32, name="tab_q")
        tab_k = keep.tile([P, TB, 2, HD], F32, name="tab_k")
        tab = (tab_q, tab_k)

        xc = {}
        wc = {}

        def load_x(g0, g1):
            t = keep.tile([P, g1 - g0, 2 * TOKENS], U8, name="xc%d" % g0, align_bytes=64)
            nc.sync.dma_start(
                out=t[:].bitcast(I32), in_=x_words[g0:g1].rearrange("g p n -> p g n").bitcast(I32)
            )
            for g in range(g0, g1):
                xc[g] = t[:, g - g0, :]

        def load_w(cb, g0, g1):
            t = keep.tile([P, g1 - g0, 2 * NB], U8, name="wc%d_%d" % (cb, g0), align_bytes=64)
            nc.sync.dma_start(
                out=t[:].bitcast(I32),
                in_=qkv_w_words[g0:g1, :, 2 * NB * cb : 2 * NB * (cb + 1)].rearrange("g p n -> p g n").bitcast(I32),
            )
            for g in range(g0, g1):
                wc[(g, cb)] = t[:, g - g0, :]

        def load_scales(plane, src):
            for r in range(4):
                nc.sync.dma_start(
                    out=plane[r:P:32, :, :].bitcast(I32),
                    in_=src[:, r:16:4, :].rearrange("g q n -> q g n").bitcast(I32),
                )

        nc.vector.memset(wrow[:], 0.0)
        nc.vector.memset(warm[:], 1.0)
        nc.vector.memset(xs[:].bitcast(I32), 0)
        nc.vector.memset(ws[0][:].bitcast(I32), 0)
        nc.vector.memset(eps[:], EPS)
        for cb in range(1, CB):
            nc.vector.memset(ws[cb][:].bitcast(I32), 0)

        load_x(0, 1)
        load_w(0, 0, 1)
        load_scales(xs, x_scales)
        load_scales(ws[0], qkv_w_scales[:, :, 0:NB])
        load_x(1, 3)
        load_w(0, 1, 3)
        load_x(3, 6)
        load_w(0, 3, 6)
        nc.sync.dma_start(out=wrow[0:1, 0:HD], in_=q_norm_w.rearrange("(o n) -> o n", o=1))
        nc.sync.dma_start(out=wrow[0:1, HD : 2 * HD], in_=k_norm_w.rearrange("(o n) -> o n", o=1))
        nc.sync.dma_start(out=cos[:], in_=freqs_cos.rearrange("(t p) d -> p t d", p=P))
        nc.sync.dma_start(out=sin[:], in_=freqs_sin.rearrange("(t p) d -> p t d", p=P))
        for cb in range(1, CB):
            load_scales(ws[cb], qkv_w_scales[:, :, NB * cb : NB * (cb + 1)])
            load_w(cb, 0, 3)
            load_w(cb, 3, 6)

        nc.scalar.activation(out=junk[:], in_=eps[:], func=ACT.Abs_reciprocal_sqrt)

        warm_ps = psum.tile([P, NB], F32, name="warm_ps", tag="acc")
        for i in range(N_WARM):
            nc.tensor.matmul(out=warm_ps[:], lhsT=warm[:, 0:P], rhs=warm[:], start=True, stop=True)

        def mm(acc, g, tb, cb, c0, n):
            nc.tensor.matmul_mx(
                out=acc,
                lhsT=xc[g][:, 2 * P * tb : 2 * P * (tb + 1)].bitcast(FP4X4),
                lhsT_scale=xs[:, g, P * tb : P * (tb + 1)],
                rhs=wc[(g, cb)][:, 2 * c0 : 2 * (c0 + n)].bitcast(FP4X4),
                rhs_scale=ws[cb][:, g, c0 : c0 + n],
                start=(g == 0),
                stop=(g == PASSES - 1),
            )

        seen_ps = psum.tile([P, NB], F32, name="seen_ps", tag="acc")
        nc.tensor.matmul_mx(
            out=seen_ps[:],
            lhsT=xc[0][:, 0 : 2 * P].bitcast(FP4X4),
            lhsT_scale=xs[:, 0, 0:P],
            rhs=xc[0][:, 0 : 2 * NB].bitcast(FP4X4),
            rhs_scale=xs[:, 0, 0:NB],
            start=True,
            stop=True,
        )

        def gains():
            gain_ps = psum.tile([P, 2 * HD], F32, name="gain_ps", tag="acc")
            nc.tensor.matmul(out=gain_ps[:], lhsT=warm[:, 0:P], rhs=wrow[:], start=True, stop=True)
            nc.vector.tensor_scalar(out=gain[:], in0=gain_ps[:], scalar1=1.0, scalar2=None, op0=ALU.add)

        def tables(which):
            for cs, trig in ((0, cos), (1, sin)):
                nc.vector.tensor_tensor(
                    out=tab[which][:, :, cs, :].rearrange("p t (h d) -> p t h d", d=HALF),
                    in0=gain[:, HD * which : HD * (which + 1)].rearrange("p (h d) -> p h d", d=HALF)
                    .unsqueeze(1).to_broadcast([P, TB, 2, HALF]),
                    in1=trig[:].unsqueeze(2).to_broadcast([P, TB, 2, HALF]),
                    op=ALU.mult,
                )

        pair = {}

        def epilogue(i, acc, tb, cb):
            which = 0 if cb < 2 else 1
            j = i % 2
            if j == 0:
                prod = work.tile([P, 2, 4, 2, HD], F32, name="prod", tag="prod")
                pair["prod"] = prod
            prod = pair["prod"]
            sq = work.tile([P, NB], F32, name="sq", tag="sq")
            ms = work.tile([P, 4], F32, name="ms", tag="ms")
            for h in range(4):
                cols = slice(HD * h, HD * (h + 1))
                nc.scalar.activation(
                    out=sq[:, cols], in_=acc[:, cols], func=ACT.Square,
                    scale=1.0 / math.sqrt(HD), accum_out=ms[:, h : h + 1],
                )
            rstd = work.tile([P, 4], F32, name="rstd", tag="rstd")
            nc.scalar.activation(out=rstd[:], in_=ms[:], func=ACT.Abs_reciprocal_sqrt, bias=eps[:, 0:1], scale=1.0)
            for h in range(4):
                cols = slice(HD * h, HD * (h + 1))
                nc.vector.scalar_tensor_tensor(
                    out=prod[:, j, h, :, :], in0=acc[:, cols].unsqueeze(1).to_broadcast([P, 2, HD]),
                    scalar=rstd[:, h : h + 1], in1=tab[which][:, tb, :, :],
                    op0=ALU.mult, op1=ALU.mult,
                )
            if j == 1:
                res = work.tile([P, 2, NB], F32, name="res", tag="res")
                r4 = res[:].rearrange("p b (h t d) -> p (b h) t d", t=2, d=HALF)
                v5 = prod[:].rearrange("p b h c (t d) -> p (b h) c t d", t=2)
                c4 = v5[:, :, 0, :, :]
                s4 = v5[:, :, 1, :, :]
                eng = nc.vector if i >= 3 * TB - 3 else nc.gpsimd
                eng.tensor_tensor(out=r4[:, :, 0, :], in0=c4[:, :, 0, :], in1=s4[:, :, 1, :], op=ALU.subtract)
                eng.tensor_tensor(out=r4[:, :, 1, :], in0=c4[:, :, 1, :], in1=s4[:, :, 0, :], op=ALU.add)
                rows = slice(P * (tb - 1), P * (tb + 1))
                if cb < 2:
                    dst = q_out[rows, NB * cb : NB * (cb + 1)]
                else:
                    dst = k_out[rows, :]
                nc.sync.dma_start(out=dst.rearrange("(b p) n -> p b n", p=P), in_=res[:])

        first = []
        for tb in range(TB):
            acc = psum.tile([P, NB], F32, name="acc", tag="acc")
            first.append(acc)
        for g in range(G_OUTER):
            for tb in range(TB):
                mm(first[tb][:], g, tb, 0, 0, NB)
            if g == G_OUTER - 1:
                gains()
                tables(0)
        for tb in range(TB):
            for g in range(G_OUTER, PASSES):
                mm(first[tb][:], g, tb, 0, 0, NB)
            epilogue(tb, first[tb], tb, 0)
        tables(1)

        for cb in (1, 2):
            for tb in range(TB):
                acc = psum.tile([P, NB], F32, name="acc", tag="acc")
                for g in range(PASSES):
                    mm(acc[:], g, tb, cb, 0, NB)
                epilogue(TB * cb + tb, acc, tb, cb)

        for tb in range(TB):
            rows = slice(P * tb, P * (tb + 1))
            widths = [NB] if tb < TB - 1 else [NB // 2, NB // 2]
            c0 = 0
            for n in widths:
                acc = psum.tile([P, n], F32, name="acc", tag="acc")
                for g in range(PASSES):
                    mm(acc[:], g, tb, 3, c0, n)
                val = vals.tile([P, n], F32, name="val", tag="val")
                nc.scalar.copy(out=val[:], in_=acc[:])
                nc.scalar.dma_start(out=v_out[rows, c0 : c0 + n], in_=val[:])
                c0 += n
